import numpy as np
import ml_dtypes


def mxq(x, axis, fmt="e4m3"):
    dtype, down = {"e4m3": (ml_dtypes.float8_e4m3fn, 7), "e5m2": (ml_dtypes.float8_e5m2, 14)}[fmt]
    v = np.moveaxis(np.asarray(x, np.float32).astype(ml_dtypes.bfloat16).astype(np.float64), axis, -1)
    blocks = v.reshape(v.shape[:-1] + (-1, 32))
    amax = np.abs(blocks).max(-1, keepdims=True)
    byte = np.maximum(np.where(amax > 0, np.frexp(amax)[1] - 1 + 127, 0) - down, 1)
    scale = np.exp2(byte - 127.0)
    codes = (blocks / scale).astype(np.float32).astype(dtype).astype(np.float64)
    return np.moveaxis((codes * scale).reshape(v.shape), -1, axis)


WIDE = False


def mx_kscale(k):
    if not WIDE:
        return np.ones(k)
    levels = np.array([10, -10, 5, -5, 0])
    a = np.random.permutation(np.resize(levels, k // 512 * 4)).reshape(k // 512, 4)
    idx = np.arange(k)
    return np.exp2(a[idx // 512, idx % 128 // 32])


BF16 = ml_dtypes.bfloat16


def bf(x):
    return np.asarray(x, np.float32).astype(BF16)


def f64(x):
    return np.asarray(x).astype(np.float64)


B, DS, HH, WW, HID, HL, REP, GRP = 2, 32, 16, 16, 1024, 1024, 8, 4
C = 2 * DS
CN = REP * C


def elu(v):
    return np.where(v > 0.0, v, np.exp(np.minimum(v, 0.0)) - 1.0)


def neighbor_sum(x):
    xp = np.pad(x, ((0, 0), (0, 0), (1, 1), (1, 1)))
    full = sum(xp[:, :, di:di + HH, dj:dj + WW] for di in range(3) for dj in range(3))
    return full - x


def to_rows(t):
    return t.transpose(0, 2, 3, 1).reshape(B * HH * WW, t.shape[1])


def to_maps(r):
    return r.reshape(B, HH, WW, r.shape[1]).transpose(0, 3, 1, 2)


def setup_inputs():
    sc = mx_kscale(CN)[::REP]
    return {"x_cat": bf(np.random.standard_normal((B, C, HH, WW)) * 0.4 * sc[None, :, None, None]),
            "w1": bf(np.random.standard_normal((HID, CN)) / np.sqrt(CN) / np.repeat(sc, REP)[None, :])}


def reference(x_cat, w1):
    nbr = neighbor_sum(f64(x_cat))
    xn = np.repeat(nbr, REP, axis=1)
    z = mxq(to_rows(xn), 1, "e4m3") @ mxq(f64(w1), 1, "e4m3").T
    return to_maps(elu(z))

@@ -1,0 +1,137 @@
+import concourse.mybir as mybir
+from concourse.masks import make_identity
+
+BF16 = mybir.dt.bfloat16
+F32 = mybir.dt.float32
+U32 = mybir.dt.uint32
+U8 = mybir.dt.uint8
+FP8X4 = mybir.dt.float8_e4m3fn_x4
+ALU = mybir.AluOpType
+ACT = mybir.ActivationFunctionType
+
+P = 128
+PACK = 4
+B, C, H, W = 2, 64, 16, 16
+PIX = H * W
+N = B * PIX
+HID = 1024
+K = 512
+COPIES = P // C
+O_TILES = HID // P
+PAIR = 2
+PAIRS = O_TILES // PAIR
+HALVES = 2
+
+FLOPS = 2 * N * K * HID
+
+
+def tile_qca_operator_deep_pa_s_kernel(tc, x_cat, w1, out):
+    nc = tc.nc
+    w_rows = w1.rearrange("(p g j) k -> p g j k", g=PAIRS, j=PAIR)
+    out_rows = out.rearrange("b (p g j) h w -> p g b (j h w)", g=PAIRS, j=PAIR)
+
+    with (
+        tc.tile_pool(name="keep", bufs=1) as keep,
+        tc.tile_pool(name="w_in", bufs=PAIRS) as w_in,
+        tc.tile_pool(name="w_grouped", bufs=2) as w_grouped,
+        tc.tile_pool(name="tail", bufs=3) as tail,
+        tc.psum_pool(name="w_psum", bufs=PAIRS) as w_psum,
+        tc.psum_pool(name="z_psum", bufs=4) as z_psum,
+    ):
+        warm = keep.tile([P, 1], F32)
+        nc.vector.memset(warm[:], 0.0)
+        nc.scalar.activation(out=warm[:], in_=warm[:], func=ACT.Exp)
+
+        ident = keep.tile([P, P], F32)
+        make_identity(nc, ident[:])
+
+        x_pad = keep.tile([P, B, H + 2, W], BF16)
+        nc.vector.memset(x_pad[:, :, 0, :], 0.0)
+        nc.vector.memset(x_pad[:, :, H + 1, :], 0.0)
+        v_pad = keep.tile([P, B, H, W + 2], F32)
+        nc.vector.memset(v_pad[:], 0.0)
+
+        for r in range(COPIES):
+            nc.sync.dma_start(
+                out=x_pad[r:P:COPIES, :, 1 : H + 1, :].rearrange("c b h w -> c b (h w)"),
+                in_=x_cat.rearrange("b c h w -> c b (h w)"),
+            )
+        w_raw = []
+        for g in range(PAIRS):
+            w_pair = w_in.tile([P, PAIR, K], BF16, name="w_pair")
+            nc.sync.dma_start(out=w_pair[:], in_=w_rows[:, g])
+            w_raw.append(w_pair)
+
+        above_below = keep.tile([P, B, H, W], F32)
+        sides = keep.tile([P, B, H, W], F32)
+        nbr = keep.tile([P, B, H, W], BF16)
+        for b in range(B):
+            nc.vector.tensor_add(
+                out=above_below[:, b], in0=x_pad[:, b, 0:H, :], in1=x_pad[:, b, 2 : H + 2, :]
+            )
+        for b in range(B):
+            nc.vector.tensor_add(
+                out=v_pad[:, b, :, 1 : W + 1], in0=above_below[:, b], in1=x_pad[:, b, 1 : H + 1, :]
+            )
+        for b in range(B):
+            nc.vector.tensor_add(
+                out=sides[:, b], in0=v_pad[:, b, :, 0:W], in1=v_pad[:, b, :, 2 : W + 2]
+            )
+        for b in range(B):
+            nc.vector.tensor_add(out=nbr[:, b], in0=sides[:, b], in1=above_below[:, b])
+
+        x_grouped = keep.tile([P, N, PACK], BF16, align_bytes=64)
+        nc.vector.tensor_copy(
+            out=x_grouped[:],
+            in_=nbr[:].rearrange("p b h w -> p (b h w)").unsqueeze(2).to_broadcast([P, N, PACK]),
+        )
+
+        w_codes = keep.tile([P, O_TILES, P], U32, align_bytes=64)
+        w_scales = keep.tile([P, O_TILES, P], U8, align_bytes=64)
+        x_codes = keep.tile([P, N], U32, align_bytes=64)
+        x_scales = keep.tile([P, N], U8, align_bytes=64)
+
+        for g in range(PAIRS):
+            w_t = w_psum.tile([P, PAIR, HALVES, P], F32, name="w_t")
+            for j in range(PAIR):
+                words = w_raw[g][:, j, :].bitcast(F32).rearrange("o (q u) -> o q u", u=HALVES)
+                for u in range(HALVES):
+                    nc.tensor.transpose(w_t[:, j, u, :], words[:, :, u], ident[:])
+            grouped = w_grouped.tile([P, PAIR, P, PACK], BF16, name="grouped", align_bytes=64)
+            nc.scalar.copy(
+                out=grouped[:].bitcast(F32), in_=w_t[:].rearrange("q j u o -> q j o u")
+            )
+            tiles = slice(g * PAIR, (g + 1) * PAIR)
+            nc.vector.quantize_mx(
+                out=w_codes[:, tiles, :].rearrange("q j o -> q (j o)").bitcast(FP8X4),
+                scales=w_scales[:, tiles, :].rearrange("q j o -> q (j o)"),
+                in_=grouped[:].rearrange("q j o t -> q (j o t)"),
+            )
+            if g == 0:
+                nc.vector.quantize_mx(
+                    out=x_codes[:].bitcast(FP8X4),
+                    scales=x_scales[:],
+                    in_=x_grouped[:].rearrange("p n t -> p (n t)"),
+                )
+
+        for g in range(PAIRS):
+            y = tail.tile([P, B, PAIR, PIX], F32, name="y")
+            for j in range(PAIR):
+                t = g * PAIR + j
+                z = z_psum.tile([P, B, PIX], F32, name="z")
+                nc.tensor.matmul_mx(
+                    out=z[:].rearrange("o b x -> o (b x)"),
+                    lhsT=w_codes[:, t, :].bitcast(FP8X4),
+                    lhsT_scale=w_scales[:, t, :],
+                    rhs=x_codes[:].bitcast(FP8X4),
+                    rhs_scale=x_scales[:],
+                    start=True,
+                    stop=True,
+                )
+                e = tail.tile([P, B, PIX], F32, name="e")
+                nc.scalar.activation(out=e[:], in_=z[:], func=ACT.Exp)
+                nc.vector.tensor_scalar(
+                    out=e[:], in0=e[:], scalar1=1.0, scalar2=-1.0, op0=ALU.min, op1=ALU.add
+                )
+                nc.vector.tensor_max(out=y[:, :, j, :], in0=z[:], in1=e[:])
+            nc.sync.dma_start(out=out_rows[:, g], in_=y[:].rearrange("o b j x -> o b (j x)"))

@@ -130,7 +130,7 @@ def tile_qca_operator_deep_pa_s_kernel(tc, x_cat, w1, out):
                 )
                 e = tail.tile([P, B, PIX], F32, name="e")
                 nc.scalar.activation(out=e[:], in_=z[:], func=ACT.Exp)
-                nc.vector.tensor_scalar(
+                nc.gpsimd.tensor_scalar(
                     out=e[:], in0=e[:], scalar1=1.0, scalar2=-1.0, op0=ALU.min, op1=ALU.add
                 )
                 nc.vector.tensor_max(out=y[:, :, j, :], in0=z[:], in1=e[:])

@@ -21,6 +21,7 @@ O_TILES = HID // P
 PAIR = 2
 PAIRS = O_TILES // PAIR
 HALVES = 2
+BANKS = 8
 
 FLOPS = 2 * N * K * HID
 
@@ -35,8 +36,7 @@ def tile_qca_operator_deep_pa_s_kernel(tc, x_cat, w1, out):
         tc.tile_pool(name="w_in", bufs=PAIRS) as w_in,
         tc.tile_pool(name="w_grouped", bufs=2) as w_grouped,
         tc.tile_pool(name="tail", bufs=3) as tail,
-        tc.psum_pool(name="w_psum", bufs=PAIRS) as w_psum,
-        tc.psum_pool(name="z_psum", bufs=4) as z_psum,
+        tc.psum_pool(name="psum", bufs=BANKS) as psum,
     ):
         warm = keep.tile([P, 1], F32)
         nc.vector.memset(warm[:], 0.0)
@@ -80,11 +80,10 @@ def tile_qca_operator_deep_pa_s_kernel(tc, x_cat, w1, out):
         for b in range(B):
             nc.vector.tensor_add(out=nbr[:, b], in0=sides[:, b], in1=above_below[:, b])
 
-        x_grouped = keep.tile([P, N, PACK], BF16, align_bytes=64)
-        nc.vector.tensor_copy(
-            out=x_grouped[:],
-            in_=nbr[:].rearrange("p b h w -> p (b h w)").unsqueeze(2).to_broadcast([P, N, PACK]),
-        )
+        x_grouped = keep.tile([P, B, PIX, PACK], BF16, align_bytes=64)
+        repeated = nbr[:].rearrange("p b h w -> p b (h w)").unsqueeze(3).to_broadcast([P, B, PIX, PACK])
+        nc.scalar.copy(out=x_grouped[:, 0], in_=repeated[:, 0])
+        nc.vector.tensor_copy(out=x_grouped[:, 1], in_=repeated[:, 1])
 
         w_codes = keep.tile([P, O_TILES, P], U32, align_bytes=64)
         w_scales = keep.tile([P, O_TILES, P], U8, align_bytes=64)
@@ -92,7 +91,7 @@ def tile_qca_operator_deep_pa_s_kernel(tc, x_cat, w1, out):
         x_scales = keep.tile([P, N], U8, align_bytes=64)
 
         for g in range(PAIRS):
-            w_t = w_psum.tile([P, PAIR, HALVES, P], F32, name="w_t")
+            w_t = psum.tile([P, PAIR, HALVES, P], F32, name="w_t", tag="bank")
             for j in range(PAIR):
                 words = w_raw[g][:, j, :].bitcast(F32).rearrange("o (q u) -> o q u", u=HALVES)
                 for u in range(HALVES):
@@ -111,14 +110,14 @@ def tile_qca_operator_deep_pa_s_kernel(tc, x_cat, w1, out):
                 nc.vector.quantize_mx(
                     out=x_codes[:].bitcast(FP8X4),
                     scales=x_scales[:],
-                    in_=x_grouped[:].rearrange("p n t -> p (n t)"),
+                    in_=x_grouped[:].rearrange("p b x t -> p (b x t)"),
                 )
 
         for g in range(PAIRS):
             y = tail.tile([P, B, PAIR, PIX], F32, name="y")
             for j in range(PAIR):
                 t = g * PAIR + j
-                z = z_psum.tile([P, B, PIX], F32, name="z")
+                z = psum.tile([P, B, PIX], F32, name="z", tag="bank")
                 nc.tensor.matmul_mx(
                     out=z[:].rearrange("o b x -> o (b x)"),
                     lhsT=w_codes[:, t, :].bitcast(FP8X4),
@@ -131,7 +130,9 @@ def tile_qca_operator_deep_pa_s_kernel(tc, x_cat, w1, out):
                 e = tail.tile([P, B, PIX], F32, name="e")
                 nc.scalar.activation(out=e[:], in_=z[:], func=ACT.Exp)
                 nc.gpsimd.tensor_scalar(
-                    out=e[:], in0=e[:], scalar1=1.0, scalar2=-1.0, op0=ALU.min, op1=ALU.add
+                    out=e[:], in0=e[:], scalar1=1.0, scalar2=-1.0, op0=ALU.mult, op1=ALU.add
                 )
-                nc.vector.tensor_max(out=y[:, :, j, :], in0=z[:], in1=e[:])
+                nc.vector.scalar_tensor_tensor(
+                    out=y[:, :, j, :], in0=e[:], scalar=0.0, in1=z[:], op0=ALU.min, op1=ALU.max
+                )
             nc.sync.dma_start(out=out_rows[:, g], in_=y[:].rearrange("o b j x -> o b (j x)"))

@@ -35,7 +35,7 @@ def tile_qca_operator_deep_pa_s_kernel(tc, x_cat, w1, out):
         tc.tile_pool(name="keep", bufs=1) as keep,
         tc.tile_pool(name="w_in", bufs=PAIRS) as w_in,
         tc.tile_pool(name="w_grouped", bufs=2) as w_grouped,
-        tc.tile_pool(name="tail", bufs=3) as tail,
+        tc.tile_pool(name="tail", bufs=O_TILES) as tail,
         tc.psum_pool(name="psum", bufs=BANKS) as psum,
     ):
         warm = keep.tile([P, 1], F32)
@@ -129,7 +129,8 @@ def tile_qca_operator_deep_pa_s_kernel(tc, x_cat, w1, out):
                 )
                 e = tail.tile([P, B, PIX], F32, name="e")
                 nc.scalar.activation(out=e[:], in_=z[:], func=ACT.Exp)
-                nc.gpsimd.tensor_scalar(
+                minus_one = nc.vector if t % 3 == 0 else nc.gpsimd
+                minus_one.tensor_scalar(
                     out=e[:], in0=e[:], scalar1=1.0, scalar2=-1.0, op0=ALU.mult, op1=ALU.add
                 )
                 nc.vector.scalar_tensor_tensor(

@@ -17,9 +17,11 @@ N = B * PIX
 HID = 1024
 K = 512
 COPIES = P // C
+ROW_HALVES = 2
 O_TILES = HID // P
 PAIR = 2
 PAIRS = O_TILES // PAIR
+EARLY_PAIRS = 1
 HALVES = 2
 BANKS = 8
 
@@ -34,7 +36,7 @@ def tile_qca_operator_deep_pa_s_kernel(tc, x_cat, w1, out):
     with (
         tc.tile_pool(name="keep", bufs=1) as keep,
         tc.tile_pool(name="w_in", bufs=PAIRS) as w_in,
-        tc.tile_pool(name="w_grouped", bufs=2) as w_grouped,
+        tc.tile_pool(name="w_grouped", bufs=PAIRS) as w_grouped,
         tc.tile_pool(name="tail", bufs=O_TILES) as tail,
         tc.psum_pool(name="psum", bufs=BANKS) as psum,
     ):
@@ -44,17 +46,22 @@ def tile_qca_operator_deep_pa_s_kernel(tc, x_cat, w1, out):
 
         ident = keep.tile([P, P], F32)
         make_identity(nc, ident[:])
+        spread = keep.tile([P, B, C, COPIES], BF16)
+        nc.gpsimd.tensor_copy(
+            out=spread[:],
+            in_=ident[:].rearrange("q (c b) -> q b c", b=B).unsqueeze(3).to_broadcast([P, B, C, COPIES]),
+        )
 
-        x_pad = keep.tile([P, B, H + 2, W], BF16)
-        nc.vector.memset(x_pad[:, :, 0, :], 0.0)
-        nc.vector.memset(x_pad[:, :, H + 1, :], 0.0)
-        v_pad = keep.tile([P, B, H, W + 2], F32)
+        x_pad = keep.tile([P, H + 2, W], BF16)
+        nc.vector.memset(x_pad[:, 0, :], 0.0)
+        nc.vector.memset(x_pad[:, H + 1, :], 0.0)
+        v_pad = keep.tile([P, H, W + 2], F32)
         nc.vector.memset(v_pad[:], 0.0)
 
-        for r in range(COPIES):
+        for b in range(B):
             nc.sync.dma_start(
-                out=x_pad[r:P:COPIES, :, 1 : H + 1, :].rearrange("c b h w -> c b (h w)"),
-                in_=x_cat.rearrange("b c h w -> c b (h w)"),
+                out=x_pad[b:P:B, 1 : H + 1, :].rearrange("c h w -> c (h w)"),
+                in_=x_cat[b].rearrange("c h w -> c (h w)"),
             )
         w_raw = []
         for g in range(PAIRS):
@@ -62,35 +69,12 @@ def tile_qca_operator_deep_pa_s_kernel(tc, x_cat, w1, out):
             nc.sync.dma_start(out=w_pair[:], in_=w_rows[:, g])
             w_raw.append(w_pair)
 
-        above_below = keep.tile([P, B, H, W], F32)
-        sides = keep.tile([P, B, H, W], F32)
-        nbr = keep.tile([P, B, H, W], BF16)
-        for b in range(B):
-            nc.vector.tensor_add(
-                out=above_below[:, b], in0=x_pad[:, b, 0:H, :], in1=x_pad[:, b, 2 : H + 2, :]
-            )
-        for b in range(B):
-            nc.vector.tensor_add(
-                out=v_pad[:, b, :, 1 : W + 1], in0=above_below[:, b], in1=x_pad[:, b, 1 : H + 1, :]
-            )
-        for b in range(B):
-            nc.vector.tensor_add(
-                out=sides[:, b], in0=v_pad[:, b, :, 0:W], in1=v_pad[:, b, :, 2 : W + 2]
-            )
-        for b in range(B):
-            nc.vector.tensor_add(out=nbr[:, b], in0=sides[:, b], in1=above_below[:, b])
-
-        x_grouped = keep.tile([P, B, PIX, PACK], BF16, align_bytes=64)
-        repeated = nbr[:].rearrange("p b h w -> p b (h w)").unsqueeze(3).to_broadcast([P, B, PIX, PACK])
-        nc.scalar.copy(out=x_grouped[:, 0], in_=repeated[:, 0])
-        nc.vector.tensor_copy(out=x_grouped[:, 1], in_=repeated[:, 1])
-
         w_codes = keep.tile([P, O_TILES, P], U32, align_bytes=64)
         w_scales = keep.tile([P, O_TILES, P], U8, align_bytes=64)
         x_codes = keep.tile([P, N], U32, align_bytes=64)
         x_scales = keep.tile([P, N], U8, align_bytes=64)
 
-        for g in range(PAIRS):
+        def transpose_pair(g):
             w_t = psum.tile([P, PAIR, HALVES, P], F32, name="w_t", tag="bank")
             for j in range(PAIR):
                 words = w_raw[g][:, j, :].bitcast(F32).rearrange("o (q u) -> o q u", u=HALVES)
@@ -100,18 +84,74 @@ def tile_qca_operator_deep_pa_s_kernel(tc, x_cat, w1, out):
             nc.scalar.copy(
                 out=grouped[:].bitcast(F32), in_=w_t[:].rearrange("q j u o -> q j o u")
             )
+            return grouped
+
+        def quantise_pair(g, grouped):
             tiles = slice(g * PAIR, (g + 1) * PAIR)
             nc.vector.quantize_mx(
                 out=w_codes[:, tiles, :].rearrange("q j o -> q (j o)").bitcast(FP8X4),
                 scales=w_scales[:, tiles, :].rearrange("q j o -> q (j o)"),
                 in_=grouped[:].rearrange("q j o t -> q (j o t)"),
             )
-            if g == 0:
-                nc.vector.quantize_mx(
-                    out=x_codes[:].bitcast(FP8X4),
-                    scales=x_scales[:],
-                    in_=x_grouped[:].rearrange("p b x t -> p (b x t)"),
-                )
+
+        early_grouped = [transpose_pair(g) for g in range(EARLY_PAIRS)]
+
+        above_below = keep.tile([P, H, W], F32)
+        sides = keep.tile([P, H, W], F32)
+        nbr = keep.tile([P, H, W], BF16)
+        row_halves = [slice(s * H // ROW_HALVES, (s + 1) * H // ROW_HALVES) for s in range(ROW_HALVES)]
+        for rows in row_halves:
+            nc.vector.tensor_add(
+                out=above_below[:, rows, :],
+                in0=x_pad[:, rows.start : rows.stop, :],
+                in1=x_pad[:, rows.start + 2 : rows.stop + 2, :],
+            )
+        for rows in row_halves:
+            nc.vector.tensor_add(
+                out=v_pad[:, rows, 1 : W + 1],
+                in0=above_below[:, rows, :],
+                in1=x_pad[:, rows.start + 1 : rows.stop + 1, :],
+            )
+        for rows in row_halves:
+            nc.vector.tensor_add(
+                out=sides[:, rows, :], in0=v_pad[:, rows, 0:W], in1=v_pad[:, rows, 2 : W + 2]
+            )
+        for rows in row_halves:
+            nc.vector.tensor_add(
+                out=nbr[:, rows, :], in0=sides[:, rows, :], in1=above_below[:, rows, :]
+            )
+
+        x_grouped = keep.tile([P, B, PIX, PACK], BF16, align_bytes=64)
+        for b in range(B):
+            both = psum.tile([P, PIX, HALVES], BF16, name="both", tag="bank")
+            nc.tensor.matmul(
+                out=both[:].rearrange("p x d -> p (x d)"),
+                lhsT=spread[:, b].rearrange("q c r -> q (c r)"),
+                rhs=nbr[:].rearrange("q h w -> q (h w)").unsqueeze(2).to_broadcast([P, PIX, HALVES]),
+                start=True,
+                stop=True,
+            )
+            twice = (
+                both[:].rearrange("p x d -> p (x d)").bitcast(F32).unsqueeze(2).to_broadcast([P, PIX, HALVES])
+            )
+            words = (
+                x_grouped[:, b].rearrange("p x t -> p (x t)").bitcast(F32).rearrange("p (x u) -> p x u", u=HALVES)
+            )
+            if b == 0:
+                nc.scalar.copy(out=words, in_=twice)
+            else:
+                nc.vector.tensor_copy(out=words, in_=twice)
+
+        quantise_pair(0, early_grouped[0])
+        nc.vector.quantize_mx(
+            out=x_codes[:].bitcast(FP8X4),
+            scales=x_scales[:],
+            in_=x_grouped[:].rearrange("p b x t -> p (b x t)"),
+        )
+        for g in range(1, EARLY_PAIRS):
+            quantise_pair(g, early_grouped[g])
+        for g in range(EARLY_PAIRS, PAIRS):
+            quantise_pair(g, transpose_pair(g))
 
         for g in range(PAIRS):
             y = tail.tile([P, B, PAIR, PIX], F32, name="y")

@@ -49,7 +49,7 @@ def tile_qca_operator_deep_pa_s_kernel(tc, x_cat, w1, out):
         spread = keep.tile([P, B, C, COPIES], BF16)
         nc.gpsimd.tensor_copy(
             out=spread[:],
-            in_=ident[:].rearrange("q (c b) -> q b c", b=B).unsqueeze(3).to_broadcast([P, B, C, COPIES]),
+            in_=ident[:].rearrange("q (b c) -> q b c", b=B).unsqueeze(3).to_broadcast([P, B, C, COPIES]),
         )
 
         x_pad = keep.tile([P, H + 2, W], BF16)
@@ -58,11 +58,10 @@ def tile_qca_operator_deep_pa_s_kernel(tc, x_cat, w1, out):
         v_pad = keep.tile([P, H, W + 2], F32)
         nc.vector.memset(v_pad[:], 0.0)
 
-        for b in range(B):
-            nc.sync.dma_start(
-                out=x_pad[b:P:B, 1 : H + 1, :].rearrange("c h w -> c (h w)"),
-                in_=x_cat[b].rearrange("c h w -> c (h w)"),
-            )
+        nc.sync.dma_start(
+            out=x_pad[:, 1 : H + 1, :].rearrange("q h w -> q (h w)"),
+            in_=x_cat.rearrange("b c h w -> (b c) (h w)"),
+        )
         w_raw = []
         for g in range(PAIRS):
             w_pair = w_in.tile([P, PAIR, K], BF16, name="w_pair")
@@ -138,16 +137,18 @@ def tile_qca_operator_deep_pa_s_kernel(tc, x_cat, w1, out):
                 x_grouped[:, b].rearrange("p x t -> p (x t)").bitcast(F32).rearrange("p (x u) -> p x u", u=HALVES)
             )
             if b == 0:
-                nc.scalar.copy(out=words, in_=twice)
-            else:
                 nc.vector.tensor_copy(out=words, in_=twice)
+            else:
+                nc.scalar.copy(out=words, in_=twice)
 
         quantise_pair(0, early_grouped[0])
-        nc.vector.quantize_mx(
-            out=x_codes[:].bitcast(FP8X4),
-            scales=x_scales[:],
-            in_=x_grouped[:].rearrange("p b x t -> p (b x t)"),
-        )
+        for b in range(B):
+            pixels = slice(b * PIX, (b + 1) * PIX)
+            nc.vector.quantize_mx(
+                out=x_codes[:, pixels].bitcast(FP8X4),
+                scales=x_scales[:, pixels],
+                in_=x_grouped[:, b].rearrange("p x t -> p (x t)"),
+            )
         for g in range(1, EARLY_PAIRS):
             quantise_pair(g, early_grouped[g])
         for g in range(EARLY_PAIRS, PAIRS):

@@ -155,26 +155,29 @@ def tile_qca_operator_deep_pa_s_kernel(tc, x_cat, w1, out):
             quantise_pair(g, transpose_pair(g))
 
         for g in range(PAIRS):
-            y = tail.tile([P, B, PAIR, PIX], F32, name="y")
-            for j in range(PAIR):
-                t = g * PAIR + j
-                z = psum.tile([P, B, PIX], F32, name="z", tag="bank")
-                nc.tensor.matmul_mx(
-                    out=z[:].rearrange("o b x -> o (b x)"),
-                    lhsT=w_codes[:, t, :].bitcast(FP8X4),
-                    lhsT_scale=w_scales[:, t, :],
-                    rhs=x_codes[:].bitcast(FP8X4),
-                    rhs_scale=x_scales[:],
-                    start=True,
-                    stop=True,
-                )
-                e = tail.tile([P, B, PIX], F32, name="e")
+            for b in range(B):
+                unit = g * B + b
+                pixels = slice(b * PIX, (b + 1) * PIX)
+                z = psum.tile([P, PAIR, PIX], F32, name="z", tag="bank")
+                for j in range(PAIR):
+                    t = g * PAIR + j
+                    nc.tensor.matmul_mx(
+                        out=z[:, j, :],
+                        lhsT=w_codes[:, t, :].bitcast(FP8X4),
+                        lhsT_scale=w_scales[:, t, :],
+                        rhs=x_codes[:, pixels].bitcast(FP8X4),
+                        rhs_scale=x_scales[:, pixels],
+                        start=True,
+                        stop=True,
+                    )
+                e = tail.tile([P, PAIR, PIX], F32, name="e")
                 nc.scalar.activation(out=e[:], in_=z[:], func=ACT.Exp)
-                minus_one = nc.vector if t % 3 == 0 else nc.gpsimd
+                minus_one = nc.vector if unit % 3 == 0 else nc.gpsimd
                 minus_one.tensor_scalar(
                     out=e[:], in0=e[:], scalar1=1.0, scalar2=-1.0, op0=ALU.mult, op1=ALU.add
                 )
+                y = tail.tile([P, PAIR, PIX], F32, name="y")
                 nc.vector.scalar_tensor_tensor(
-                    out=y[:, :, j, :], in0=e[:], scalar=0.0, in1=z[:], op0=ALU.min, op1=ALU.max
+                    out=y[:], in0=e[:], scalar=0.0, in1=z[:], op0=ALU.min, op1=ALU.max
                 )
-            nc.sync.dma_start(out=out_rows[:, g], in_=y[:].rearrange("o b j x -> o b (j x)"))
+                nc.sync.dma_start(out=out_rows[:, g, b], in_=y[:].rearrange("o j x -> o (j x)"))

@@ -23,6 +23,8 @@ PAIR = 2
 PAIRS = O_TILES // PAIR
 EARLY_PAIRS = 1
 HALVES = 2
+VECTOR_MIDDLE = (0, 3)
+SCALAR_MIDDLE = (6, 7)
 BANKS = 8
 
 FLOPS = 2 * N * K * HID
@@ -73,16 +75,14 @@ def tile_qca_operator_deep_pa_s_kernel(tc, x_cat, w1, out):
         x_codes = keep.tile([P, N], U32, align_bytes=64)
         x_scales = keep.tile([P, N], U8, align_bytes=64)
 
-        def transpose_pair(g):
+        def transpose_pair(g, copier):
             w_t = psum.tile([P, PAIR, HALVES, P], F32, name="w_t", tag="bank")
             for j in range(PAIR):
                 words = w_raw[g][:, j, :].bitcast(F32).rearrange("o (q u) -> o q u", u=HALVES)
                 for u in range(HALVES):
                     nc.tensor.transpose(w_t[:, j, u, :], words[:, :, u], ident[:])
             grouped = w_grouped.tile([P, PAIR, P, PACK], BF16, name="grouped", align_bytes=64)
-            nc.scalar.copy(
-                out=grouped[:].bitcast(F32), in_=w_t[:].rearrange("q j u o -> q j o u")
-            )
+            copier(out=grouped[:].bitcast(F32), in_=w_t[:].rearrange("q j u o -> q j o u"))
             return grouped
 
         def quantise_pair(g, grouped):
@@ -93,7 +93,7 @@ def tile_qca_operator_deep_pa_s_kernel(tc, x_cat, w1, out):
                 in_=grouped[:].rearrange("q j o t -> q (j o t)"),
             )
 
-        early_grouped = [transpose_pair(g) for g in range(EARLY_PAIRS)]
+        early_grouped = [transpose_pair(g, nc.scalar.copy) for g in range(EARLY_PAIRS)]
 
         above_below = keep.tile([P, H, W], F32)
         sides = keep.tile([P, H, W], F32)
@@ -149,35 +149,63 @@ def tile_qca_operator_deep_pa_s_kernel(tc, x_cat, w1, out):
                 scales=x_scales[:, pixels],
                 in_=x_grouped[:, b].rearrange("p x t -> p (x t)"),
             )
-        for g in range(1, EARLY_PAIRS):
-            quantise_pair(g, early_grouped[g])
-        for g in range(EARLY_PAIRS, PAIRS):
-            quantise_pair(g, transpose_pair(g))
+        grouped_1 = transpose_pair(1, nc.scalar.copy)
+        grouped_2 = transpose_pair(2, nc.scalar.copy)
+        quantise_pair(1, grouped_1)
+        grouped_3 = transpose_pair(3, nc.vector.tensor_copy)
+        quantise_pair(2, grouped_2)
+        quantise_pair(3, grouped_3)
 
-        for g in range(PAIRS):
-            for b in range(B):
-                unit = g * B + b
-                pixels = slice(b * PIX, (b + 1) * PIX)
-                z = psum.tile([P, PAIR, PIX], F32, name="z", tag="bank")
-                for j in range(PAIR):
-                    t = g * PAIR + j
-                    nc.tensor.matmul_mx(
-                        out=z[:, j, :],
-                        lhsT=w_codes[:, t, :].bitcast(FP8X4),
-                        lhsT_scale=w_scales[:, t, :],
-                        rhs=x_codes[:, pixels].bitcast(FP8X4),
-                        rhs_scale=x_scales[:, pixels],
-                        start=True,
-                        stop=True,
-                    )
-                e = tail.tile([P, PAIR, PIX], F32, name="e")
-                nc.scalar.activation(out=e[:], in_=z[:], func=ACT.Exp)
-                minus_one = nc.vector if unit % 3 == 0 else nc.gpsimd
-                minus_one.tensor_scalar(
+        UNITS = PAIRS * B
+        z_of, e_of = {}, {}
+
+        def matmuls_and_exp(unit):
+            g, b = divmod(unit, B)
+            pixels = slice(b * PIX, (b + 1) * PIX)
+            z = psum.tile([P, PAIR, PIX], F32, name="z", tag="bank")
+            for j in range(PAIR):
+                t = g * PAIR + j
+                nc.tensor.matmul_mx(
+                    out=z[:, j, :],
+                    lhsT=w_codes[:, t, :].bitcast(FP8X4),
+                    lhsT_scale=w_scales[:, t, :],
+                    rhs=x_codes[:, pixels].bitcast(FP8X4),
+                    rhs_scale=x_scales[:, pixels],
+                    start=True,
+                    stop=True,
+                )
+            e = tail.tile([P, PAIR, PIX], F32, name="e")
+            nc.scalar.activation(out=e[:], in_=z[:], func=ACT.Exp)
+            z_of[unit], e_of[unit] = z, e
+
+        def middle_pass(unit):
+            e = e_of[unit]
+            if unit in SCALAR_MIDDLE:
+                nc.scalar.activation(out=e[:], in_=e[:], func=ACT.Relu, scale=-1.0, bias=1.0)
+            else:
+                engine = nc.vector if unit in VECTOR_MIDDLE else nc.gpsimd
+                engine.tensor_scalar(
                     out=e[:], in0=e[:], scalar1=1.0, scalar2=-1.0, op0=ALU.mult, op1=ALU.add
                 )
-                y = tail.tile([P, PAIR, PIX], F32, name="y")
+
+        def last_pass_and_store(unit):
+            g, b = divmod(unit, B)
+            z, e = z_of[unit], e_of[unit]
+            y = tail.tile([P, PAIR, PIX], F32, name="y")
+            if unit in SCALAR_MIDDLE:
+                nc.vector.scalar_tensor_tensor(
+                    out=y[:], in0=z[:], scalar=0.0, in1=e[:], op0=ALU.max, op1=ALU.subtract
+                )
+            else:
                 nc.vector.scalar_tensor_tensor(
                     out=y[:], in0=e[:], scalar=0.0, in1=z[:], op0=ALU.min, op1=ALU.max
                 )
-                nc.sync.dma_start(out=out_rows[:, g, b], in_=y[:].rearrange("o j x -> o (j x)"))
+            nc.sync.dma_start(out=out_rows[:, g, b], in_=y[:].rearrange("o j x -> o (j x)"))
+
+        for step in range(UNITS + 2):
+            if step < UNITS:
+                matmuls_and_exp(step)
+            if 0 <= step - 1 < UNITS:
+                middle_pass(step - 1)
+            if 0 <= step - 2 < UNITS:
+                last_pass_and_store(step - 2)

@@ -21,7 +21,6 @@ ROW_HALVES = 2
 O_TILES = HID // P
 PAIR = 2
 PAIRS = O_TILES // PAIR
-EARLY_PAIRS = 1
 HALVES = 2
 VECTOR_MIDDLE = (0, 3)
 SCALAR_MIDDLE = (6, 7)
@@ -75,25 +74,30 @@ def tile_qca_operator_deep_pa_s_kernel(tc, x_cat, w1, out):
         x_codes = keep.tile([P, N], U32, align_bytes=64)
         x_scales = keep.tile([P, N], U8, align_bytes=64)
 
-        def transpose_pair(g, copier):
-            w_t = psum.tile([P, PAIR, HALVES, P], F32, name="w_t", tag="bank")
-            for j in range(PAIR):
-                words = w_raw[g][:, j, :].bitcast(F32).rearrange("o (q u) -> o q u", u=HALVES)
+        grouped_of = [
+            w_grouped.tile([P, PAIR, P, PACK], BF16, name="grouped", align_bytes=64) for g in range(PAIRS)
+        ]
+
+        def transpose_tiles(g, tiles, copier):
+            count = tiles.stop - tiles.start
+            w_t = psum.tile([P, count, HALVES, P], F32, name="w_t", tag="bank")
+            for j in range(count):
+                words = w_raw[g][:, tiles.start + j, :].bitcast(F32).rearrange("o (q u) -> o q u", u=HALVES)
                 for u in range(HALVES):
                     nc.tensor.transpose(w_t[:, j, u, :], words[:, :, u], ident[:])
-            grouped = w_grouped.tile([P, PAIR, P, PACK], BF16, name="grouped", align_bytes=64)
-            copier(out=grouped[:].bitcast(F32), in_=w_t[:].rearrange("q j u o -> q j o u"))
-            return grouped
+            copier(out=grouped_of[g][:, tiles].bitcast(F32), in_=w_t[:].rearrange("q j u o -> q j o u"))
 
-        def quantise_pair(g, grouped):
+        def quantise_pair(g):
             tiles = slice(g * PAIR, (g + 1) * PAIR)
             nc.vector.quantize_mx(
                 out=w_codes[:, tiles, :].rearrange("q j o -> q (j o)").bitcast(FP8X4),
                 scales=w_scales[:, tiles, :].rearrange("q j o -> q (j o)"),
-                in_=grouped[:].rearrange("q j o t -> q (j o t)"),
+                in_=grouped_of[g][:].rearrange("q j o t -> q (j o t)"),
             )
 
-        early_grouped = [transpose_pair(g, nc.scalar.copy) for g in range(EARLY_PAIRS)]
+        transpose_tiles(0, slice(0, 1), nc.scalar.copy)
+        transpose_tiles(0, slice(1, 2), nc.scalar.copy)
+        transpose_tiles(1, slice(0, 1), nc.scalar.copy)
 
         above_below = keep.tile([P, H, W], F32)
         sides = keep.tile([P, H, W], F32)
@@ -120,6 +124,8 @@ def tile_qca_operator_deep_pa_s_kernel(tc, x_cat, w1, out):
                 out=nbr[:, rows, :], in0=sides[:, rows, :], in1=above_below[:, rows, :]
             )
 
+        quantise_pair(0)
+
         x_grouped = keep.tile([P, B, PIX, PACK], BF16, align_bytes=64)
         for b in range(B):
             both = psum.tile([P, PIX, HALVES], BF16, name="both", tag="bank")
@@ -141,7 +147,6 @@ def tile_qca_operator_deep_pa_s_kernel(tc, x_cat, w1, out):
             else:
                 nc.scalar.copy(out=words, in_=twice)
 
-        quantise_pair(0, early_grouped[0])
         for b in range(B):
             pixels = slice(b * PIX, (b + 1) * PIX)
             nc.vector.quantize_mx(
@@ -149,12 +154,12 @@ def tile_qca_operator_deep_pa_s_kernel(tc, x_cat, w1, out):
                 scales=x_scales[:, pixels],
                 in_=x_grouped[:, b].rearrange("p x t -> p (x t)"),
             )
-        grouped_1 = transpose_pair(1, nc.scalar.copy)
-        grouped_2 = transpose_pair(2, nc.scalar.copy)
-        quantise_pair(1, grouped_1)
-        grouped_3 = transpose_pair(3, nc.vector.tensor_copy)
-        quantise_pair(2, grouped_2)
-        quantise_pair(3, grouped_3)
+        transpose_tiles(1, slice(1, 2), nc.scalar.copy)
+        transpose_tiles(2, slice(0, PAIR), nc.scalar.copy)
+        quantise_pair(1)
+        transpose_tiles(3, slice(0, PAIR), nc.vector.tensor_copy)
+        quantise_pair(2)
+        quantise_pair(3)
 
         UNITS = PAIRS * B
         z_of, e_of = {}, {}

@@ -24,6 +24,8 @@ PAIRS = O_TILES // PAIR
 HALVES = 2
 VECTOR_MIDDLE = (0, 3)
 SCALAR_MIDDLE = (6, 7)
+WARM_MATMULS = 2
+WARM_COPIES = 2
 BANKS = 8
 
 FLOPS = 2 * N * K * HID
@@ -47,6 +49,15 @@ def tile_qca_operator_deep_pa_s_kernel(tc, x_cat, w1, out):
 
         ident = keep.tile([P, P], F32)
         make_identity(nc, ident[:])
+        warm_up = psum.tile([P, WARM_COPIES, P], F32, name="warm_up", tag="bank")
+        for i in range(WARM_MATMULS):
+            nc.tensor.matmul(
+                out=warm_up[:].rearrange("p a n -> p (a n)"),
+                lhsT=ident[:],
+                rhs=ident[:].unsqueeze(1).to_broadcast([P, WARM_COPIES, P]),
+                start=True,
+                stop=True,
+            )
         spread = keep.tile([P, B, C, COPIES], BF16)
         nc.gpsimd.tensor_copy(
             out=spread[:],

@@ -43,21 +43,24 @@ def tile_qca_operator_deep_pa_s_kernel(tc, x_cat, w1, out):
         tc.tile_pool(name="tail", bufs=O_TILES) as tail,
         tc.psum_pool(name="psum", bufs=BANKS) as psum,
     ):
+        zeros = keep.tile([P, P], F32)
+        nc.vector.memset(zeros[:], 0.0)
+        warm_up = psum.tile([P, WARM_COPIES, P], F32, name="warm_up", tag="bank")
+        for i in range(WARM_MATMULS):
+            nc.tensor.matmul(
+                out=warm_up[:].rearrange("p a n -> p (a n)"),
+                lhsT=zeros[:],
+                rhs=zeros[:].unsqueeze(1).to_broadcast([P, WARM_COPIES, P]),
+                start=True,
+                stop=True,
+            )
+
         warm = keep.tile([P, 1], F32)
         nc.vector.memset(warm[:], 0.0)
         nc.scalar.activation(out=warm[:], in_=warm[:], func=ACT.Exp)
 
         ident = keep.tile([P, P], F32)
         make_identity(nc, ident[:])
-        warm_up = psum.tile([P, WARM_COPIES, P], F32, name="warm_up", tag="bank")
-        for i in range(WARM_MATMULS):
-            nc.tensor.matmul(
-                out=warm_up[:].rearrange("p a n -> p (a n)"),
-                lhsT=ident[:],
-                rhs=ident[:].unsqueeze(1).to_broadcast([P, WARM_COPIES, P]),
-                start=True,
-                stop=True,
-            )
         spread = keep.tile([P, B, C, COPIES], BF16)
         nc.gpsimd.tensor_copy(
             out=spread[:],

@@ -33,8 +33,8 @@ FLOPS = 2 * N * K * HID
 
 def tile_qca_operator_deep_pa_s_kernel(tc, x_cat, w1, out):
     nc = tc.nc
-    w_rows = w1.rearrange("(p g j) k -> p g j k", g=PAIRS, j=PAIR)
-    out_rows = out.rearrange("b (p g j) h w -> p g b (j h w)", g=PAIRS, j=PAIR)
+    w_rows = w1.rearrange("(g p j) k -> p g j k", g=PAIRS, j=PAIR)
+    out_rows = out.rearrange("b (g p j) h w -> p g b (j h w)", g=PAIRS, j=PAIR)
 
     with (
         tc.tile_pool(name="keep", bufs=1) as keep,

import concourse.mybir as mybir
from concourse.masks import make_identity

BF16 = mybir.dt.bfloat16
F32 = mybir.dt.float32
U32 = mybir.dt.uint32
U8 = mybir.dt.uint8
FP8X4 = mybir.dt.float8_e4m3fn_x4
ALU = mybir.AluOpType
ACT = mybir.ActivationFunctionType

P = 128
PACK = 4
B, C, H, W = 2, 64, 16, 16
PIX = H * W
N = B * PIX
HID = 1024
K = 512
COPIES = P // C
ROW_HALVES = 2
O_TILES = HID // P
PAIR = 2
PAIRS = O_TILES // PAIR
HALVES = 2
VECTOR_MIDDLE = (0, 3)
SCALAR_MIDDLE = (6, 7)
WARM_MATMULS = 2
WARM_COPIES = 2
BANKS = 8

FLOPS = 2 * N * K * HID


def tile_qca_operator_deep_pa_s_kernel(tc, x_cat, w1, out):
    nc = tc.nc
    w_rows = w1.rearrange("(g p j) k -> p g j k", g=PAIRS, j=PAIR)
    out_rows = out.rearrange("b (g p j) h w -> p g b (j h w)", g=PAIRS, j=PAIR)

    with (
        tc.tile_pool(name="keep", bufs=1) as keep,
        tc.tile_pool(name="w_in", bufs=PAIRS) as w_in,
        tc.tile_pool(name="w_grouped", bufs=PAIRS) as w_grouped,
        tc.tile_pool(name="tail", bufs=O_TILES) as tail,
        tc.psum_pool(name="psum", bufs=BANKS) as psum,
    ):
        zeros = keep.tile([P, P], F32)
        nc.vector.memset(zeros[:], 0.0)
        warm_up = psum.tile([P, WARM_COPIES, P], F32, name="warm_up", tag="bank")
        for i in range(WARM_MATMULS):
            nc.tensor.matmul(
                out=warm_up[:].rearrange("p a n -> p (a n)"),
                lhsT=zeros[:],
                rhs=zeros[:].unsqueeze(1).to_broadcast([P, WARM_COPIES, P]),
                start=True,
                stop=True,
            )

        warm = keep.tile([P, 1], F32)
        nc.vector.memset(warm[:], 0.0)
        nc.scalar.activation(out=warm[:], in_=warm[:], func=ACT.Exp)

        ident = keep.tile([P, P], F32)
        make_identity(nc, ident[:])
        spread = keep.tile([P, B, C, COPIES], BF16)
        nc.gpsimd.tensor_copy(
            out=spread[:],
            in_=ident[:].rearrange("q (b c) -> q b c", b=B).unsqueeze(3).to_broadcast([P, B, C, COPIES]),
        )

        x_pad = keep.tile([P, H + 2, W], BF16)
        nc.vector.memset(x_pad[:, 0, :], 0.0)
        nc.vector.memset(x_pad[:, H + 1, :], 0.0)
        v_pad = keep.tile([P, H, W + 2], F32)
        nc.vector.memset(v_pad[:], 0.0)

        nc.sync.dma_start(
            out=x_pad[:, 1 : H + 1, :].rearrange("q h w -> q (h w)"),
            in_=x_cat.rearrange("b c h w -> (b c) (h w)"),
        )
        w_raw = []
        for g in range(PAIRS):
            w_pair = w_in.tile([P, PAIR, K], BF16, name="w_pair")
            nc.sync.dma_start(out=w_pair[:], in_=w_rows[:, g])
            w_raw.append(w_pair)

        w_codes = keep.tile([P, O_TILES, P], U32, align_bytes=64)
        w_scales = keep.tile([P, O_TILES, P], U8, align_bytes=64)
        x_codes = keep.tile([P, N], U32, align_bytes=64)
        x_scales = keep.tile([P, N], U8, align_bytes=64)

        grouped_of = [
            w_grouped.tile([P, PAIR, P, PACK], BF16, name="grouped", align_bytes=64) for g in range(PAIRS)
        ]

        def transpose_tiles(g, tiles, copier):
            count = tiles.stop - tiles.start
            w_t = psum.tile([P, count, HALVES, P], F32, name="w_t", tag="bank")
            for j in range(count):
                words = w_raw[g][:, tiles.start + j, :].bitcast(F32).rearrange("o (q u) -> o q u", u=HALVES)
                for u in range(HALVES):
                    nc.tensor.transpose(w_t[:, j, u, :], words[:, :, u], ident[:])
            copier(out=grouped_of[g][:, tiles].bitcast(F32), in_=w_t[:].rearrange("q j u o -> q j o u"))

        def quantise_pair(g):
            tiles = slice(g * PAIR, (g + 1) * PAIR)
            nc.vector.quantize_mx(
                out=w_codes[:, tiles, :].rearrange("q j o -> q (j o)").bitcast(FP8X4),
                scales=w_scales[:, tiles, :].rearrange("q j o -> q (j o)"),
                in_=grouped_of[g][:].rearrange("q j o t -> q (j o t)"),
            )

        transpose_tiles(0, slice(0, 1), nc.scalar.copy)
        transpose_tiles(0, slice(1, 2), nc.scalar.copy)
        transpose_tiles(1, slice(0, 1), nc.scalar.copy)

        above_below = keep.tile([P, H, W], F32)
        sides = keep.tile([P, H, W], F32)
        nbr = keep.tile([P, H, W], BF16)
        row_halves = [slice(s * H // ROW_HALVES, (s + 1) * H // ROW_HALVES) for s in range(ROW_HALVES)]
        for rows in row_halves:
            nc.vector.tensor_add(
                out=above_below[:, rows, :],
                in0=x_pad[:, rows.start : rows.stop, :],
                in1=x_pad[:, rows.start + 2 : rows.stop + 2, :],
            )
        for rows in row_halves:
            nc.vector.tensor_add(
                out=v_pad[:, rows, 1 : W + 1],
                in0=above_below[:, rows, :],
                in1=x_pad[:, rows.start + 1 : rows.stop + 1, :],
            )
        for rows in row_halves:
            nc.vector.tensor_add(
                out=sides[:, rows, :], in0=v_pad[:, rows, 0:W], in1=v_pad[:, rows, 2 : W + 2]
            )
        for rows in row_halves:
            nc.vector.tensor_add(
                out=nbr[:, rows, :], in0=sides[:, rows, :], in1=above_below[:, rows, :]
            )

        quantise_pair(0)

        x_grouped = keep.tile([P, B, PIX, PACK], BF16, align_bytes=64)
        for b in range(B):
            both = psum.tile([P, PIX, HALVES], BF16, name="both", tag="bank")
            nc.tensor.matmul(
                out=both[:].rearrange("p x d -> p (x d)"),
                lhsT=spread[:, b].rearrange("q c r -> q (c r)"),
                rhs=nbr[:].rearrange("q h w -> q (h w)").unsqueeze(2).to_broadcast([P, PIX, HALVES]),
                start=True,
                stop=True,
            )
            twice = (
                both[:].rearrange("p x d -> p (x d)").bitcast(F32).unsqueeze(2).to_broadcast([P, PIX, HALVES])
            )
            words = (
                x_grouped[:, b].rearrange("p x t -> p (x t)").bitcast(F32).rearrange("p (x u) -> p x u", u=HALVES)
            )
            if b == 0:
                nc.vector.tensor_copy(out=words, in_=twice)
            else:
                nc.scalar.copy(out=words, in_=twice)

        for b in range(B):
            pixels = slice(b * PIX, (b + 1) * PIX)
            nc.vector.quantize_mx(
                out=x_codes[:, pixels].bitcast(FP8X4),
                scales=x_scales[:, pixels],
                in_=x_grouped[:, b].rearrange("p x t -> p (x t)"),
            )
        transpose_tiles(1, slice(1, 2), nc.scalar.copy)
        transpose_tiles(2, slice(0, PAIR), nc.scalar.copy)
        quantise_pair(1)
        transpose_tiles(3, slice(0, PAIR), nc.vector.tensor_copy)
        quantise_pair(2)
        quantise_pair(3)

        UNITS = PAIRS * B
        z_of, e_of = {}, {}

        def matmuls_and_exp(unit):
            g, b = divmod(unit, B)
            pixels = slice(b * PIX, (b + 1) * PIX)
            z = psum.tile([P, PAIR, PIX], F32, name="z", tag="bank")
            for j in range(PAIR):
                t = g * PAIR + j
                nc.tensor.matmul_mx(
                    out=z[:, j, :],
                    lhsT=w_codes[:, t, :].bitcast(FP8X4),
                    lhsT_scale=w_scales[:, t, :],
                    rhs=x_codes[:, pixels].bitcast(FP8X4),
                    rhs_scale=x_scales[:, pixels],
                    start=True,
                    stop=True,
                )
            e = tail.tile([P, PAIR, PIX], F32, name="e")
            nc.scalar.activation(out=e[:], in_=z[:], func=ACT.Exp)
            z_of[unit], e_of[unit] = z, e

        def middle_pass(unit):
            e = e_of[unit]
            if unit in SCALAR_MIDDLE:
                nc.scalar.activation(out=e[:], in_=e[:], func=ACT.Relu, scale=-1.0, bias=1.0)
            else:
                engine = nc.vector if unit in VECTOR_MIDDLE else nc.gpsimd
                engine.tensor_scalar(
                    out=e[:], in0=e[:], scalar1=1.0, scalar2=-1.0, op0=ALU.mult, op1=ALU.add
                )

        def last_pass_and_store(unit):
            g, b = divmod(unit, B)
            z, e = z_of[unit], e_of[unit]
            y = tail.tile([P, PAIR, PIX], F32, name="y")
            if unit in SCALAR_MIDDLE:
                nc.vector.scalar_tensor_tensor(
                    out=y[:], in0=z[:], scalar=0.0, in1=e[:], op0=ALU.max, op1=ALU.subtract
                )
            else:
                nc.vector.scalar_tensor_tensor(
                    out=y[:], in0=e[:], scalar=0.0, in1=z[:], op0=ALU.min, op1=ALU.max
                )
            nc.sync.dma_start(out=out_rows[:, g, b], in_=y[:].rearrange("o j x -> o (j x)"))

        for step in range(UNITS + 2):
            if step < UNITS:
                matmuls_and_exp(step)
            if 0 <= step - 1 < UNITS:
                middle_pass(step - 1)
            if 0 <= step - 2 < UNITS:
                last_pass_and_store(step - 2)
